import numpy as np
import ml_dtypes


BF16 = ml_dtypes.bfloat16


def bf(x):
    return np.asarray(x, np.float32).astype(BF16)


def f64(x):
    return np.asarray(x).astype(np.float64)


E2M1 = np.array([0.0, 0.5, 1.0, 1.5, 2.0, 3.0, 4.0, 6.0, -0.0, -0.5, -1.0, -1.5, -2.0, -3.0, -4.0, -6.0])


def pack_weight(w, fmt):
    k, n = w.shape
    w = f64(bf(w)).reshape(k // 32, 32, n)
    amax = np.abs(w).max(1)
    if fmt == "e4m3":
        byte = np.frexp(amax)[1] - 1 + 127 - 7
    else:
        mant, ex = np.frexp(amax / 6.0)
        byte = np.where(mant > 0.5, ex, ex - 1) + 127
    byte = np.clip(np.where(amax > 0, byte, 1), 1, 254)
    scaled = (w * np.exp2(127.0 - byte)[:, None, :]).reshape(k, n).astype(np.float32)
    by_word = np.ascontiguousarray(scaled.reshape(k // 512, 128, 4, n).transpose(0, 1, 3, 2))
    if fmt == "e4m3":
        words = by_word.astype(ml_dtypes.float8_e4m3fn).view(np.uint8)
    else:
        c = by_word.astype(ml_dtypes.float4_e2m1fn).view(np.uint8) & 0xF
        words = c[..., 0::2] | (c[..., 1::2] << 4)
    return np.ascontiguousarray(words), np.ascontiguousarray(byte.astype(np.uint8).reshape(k // 512, 16, n))


def unpack_weight(words, scales, fmt):
    g, p, n, _ = words.shape
    if fmt == "e4m3":
        vals = np.ascontiguousarray(words).view(ml_dtypes.float8_e4m3fn).astype(np.float64)
    else:
        nib = np.empty((g, p, n, 4), np.uint8)
        nib[..., 0::2] = words & 0xF
        nib[..., 1::2] = words >> 4
        vals = E2M1[nib]
    vals = vals * np.repeat(np.exp2(scales.astype(np.float64) - 127.0), 8, axis=1)[..., None]
    return vals.transpose(0, 1, 3, 2).reshape(g * 512, n)

def pack4(w):
    words, scales = pack_weight(w, "e2m1")
    return words.reshape(words.shape[0], 128, -1), scales


def unpack4(words, scales):
    return unpack_weight(words.reshape(words.shape[0], 128, -1, 2), scales, "e2m1")


def kspread(k):
    return np.exp2(np.repeat(np.random.randint(-6, 7, k // 32), 32).astype(np.float64))


B, S, E, H, KVH, HD = 1, 384, 4096, 16, 4, 128
THETA = 10000.0


def apply_rope(t, cos, sin):
    x1, x2 = np.split(t, 2, axis=-1)
    c = cos[None, None, :, :]
    s = sin[None, None, :, :]
    return np.concatenate([x1 * c - x2 * s, x2 * c + x1 * s], axis=-1)


def setup_inputs():
    s = kspread(E)
    inv_freq = 1.0 / THETA ** (np.arange(0, HD, 2) / HD)
    pos = np.random.randint(0, S) + np.arange(S)
    ang = pos[:, None] * inv_freq[None, :]
    x = np.random.standard_normal((B, S, E)) * s
    x_words, x_scales = pack4(np.ascontiguousarray(x.reshape(B * S, E).T))
    Wq = np.random.standard_normal((H * HD, E)) * 1.3 / np.sqrt(E) / s[None, :]
    Wq_words, Wq_scales = pack4(np.ascontiguousarray(Wq.T))
    bq = bf(np.random.standard_normal(H * HD) * 0.3)
    Wkv = np.random.standard_normal((2 * KVH * HD, E)) * 1.3 / np.sqrt(E) / s[None, :]
    Wkv_words, Wkv_scales = pack4(np.ascontiguousarray(Wkv.T))
    bkv = bf(np.random.standard_normal(2 * KVH * HD) * 0.3)
    return {"x_words": x_words,
            "x_scales": x_scales,
            "Wq_words": Wq_words,
            "Wq_scales": Wq_scales,
            "bq": bq,
            "Wkv_words": Wkv_words,
            "Wkv_scales": Wkv_scales,
            "bkv": bkv,
            "cos": bf(np.cos(ang)),
            "sin": bf(np.sin(ang))}


def reference(x_words, x_scales, Wq_words, Wq_scales, bq, Wkv_words, Wkv_scales, bkv, cos, sin):
    xq = unpack4(x_words, x_scales).T.reshape(B, S, E)
    q = (xq @ unpack4(Wq_words, Wq_scales)) + f64(bq)
    kv = (xq @ unpack4(Wkv_words, Wkv_scales)) + f64(bkv)
    k, v = np.split(kv, 2, axis=-1)
    q = q.reshape(B, S, H, HD).transpose(0, 2, 1, 3)
    k = k.reshape(B, S, KVH, HD).transpose(0, 2, 1, 3)
    v = v.reshape(B, S, KVH, HD).transpose(0, 2, 1, 3)
    q_rot = apply_rope(q, f64(cos), f64(sin))
    k_rot = apply_rope(k, f64(cos), f64(sin))
    return q_rot, k_rot, v

@@ -1,0 +1,182 @@
+from contextlib import ExitStack
+
+import concourse.mybir as mybir
+from concourse.masks import make_identity
+
+F32 = mybir.dt.float32
+BF16 = mybir.dt.bfloat16
+I32 = mybir.dt.int32
+U8 = mybir.dt.uint8
+FP4X4 = mybir.dt.float4_e2m1fn_x4
+ADD = mybir.AluOpType.add
+MULT = mybir.AluOpType.mult
+
+P = 128
+PASSES = 8
+TOKENS = 384
+TILES = 3
+NB = 512
+HEADS = 4
+HD = 128
+HALF = 64
+Q_BLOCKS = 4
+ROPE_BLOCKS = 5
+BLOCKS = 6
+SPLITS = ((0, 1), (1, 4), (4, 8))
+
+FLOPS = 2 * TOKENS * 4096 * 3072
+
+
+def tile_qwen2attention_pa_kernel(
+    tc, x_words, x_scales, wq_words, wq_scales, bq, wkv_words, wkv_scales, bkv, cos, sin, out_q, out_k, out_v
+):
+    nc = tc.nc
+    with ExitStack() as ctx:
+        keep = ctx.enter_context(tc.tile_pool(name="keep", bufs=1))
+        work = ctx.enter_context(tc.tile_pool(name="work", bufs=2))
+        outs = ctx.enter_context(tc.tile_pool(name="outs", bufs=6))
+        psum = ctx.enter_context(tc.psum_pool(name="psum", bufs=8))
+        ctx.enter_context(tc.manual_schedule())
+
+        def load_codes(tile, words, g0, g1, c0, c1):
+            nc.sync.dma_start(out=tile[:], in_=words[g0:g1, :, 2 * c0 : 2 * c1].rearrange("g p c -> p g c"))
+
+        def load_scales(plane, scales, c0, c1):
+            for quad in range(4):
+                nc.sync.dma_start(
+                    out=plane[32 * quad : 32 * quad + 4, :, :].bitcast(I32),
+                    in_=scales[:, 4 * quad : 4 * quad + 4, c0:c1].rearrange("g r n -> r g n").bitcast(I32),
+                )
+
+        bias_rows = keep.tile([P, NB], BF16, name="bias_rows")
+        ident = keep.tile([P, P], BF16, name="ident")
+        x_plane = keep.tile([P, PASSES, TOKENS], U8, name="x_plane", align_bytes=64)
+        groups = (
+            (wq_words, wq_scales, 0, 512),
+            (wq_words, wq_scales, 512, 1024),
+            (wq_words, wq_scales, 1024, 2048),
+            (wkv_words, wkv_scales, 0, 1024),
+        )
+        planes = []
+        for i, (words, scales, c0, c1) in enumerate(groups):
+            plane = keep.tile([P, PASSES, c1 - c0], U8, name=f"plane{i}", align_bytes=64)
+            planes.append(plane)
+
+        nc.vector.memset(bias_rows[:], 0.0)
+        nc.vector.memset(x_plane[:].bitcast(I32), 0)
+        for plane in planes:
+            nc.vector.memset(plane[:].bitcast(I32), 0)
+
+        nc.gpsimd.dma_start(out=bias_rows[0:4, :], in_=bq.rearrange("(j n) -> j n", n=NB))
+        nc.gpsimd.dma_start(out=bias_rows[4:6, :], in_=bkv.rearrange("(j n) -> j n", n=NB))
+        make_identity(nc, ident[:])
+        cos_sb = keep.tile([P, TILES, HALF], BF16, name="cos_sb")
+        sin_sb = keep.tile([P, TILES, HALF], BF16, name="sin_sb")
+        nc.gpsimd.dma_start(out=cos_sb[:], in_=cos.rearrange("(m p) d -> p m d", p=P))
+        nc.gpsimd.dma_start(out=sin_sb[:], in_=sin.rearrange("(m p) d -> p m d", p=P))
+
+        x_codes = {}
+        w_codes = {}
+        for s, (g0, g1) in enumerate(SPLITS):
+            xt = keep.tile([P, g1 - g0, 2 * TOKENS], U8, name=f"x_codes{s}", align_bytes=64)
+            wt = keep.tile([P, g1 - g0, 2 * 512], U8, name=f"w_codes0_{s}", align_bytes=64)
+            load_codes(xt, x_words, g0, g1, 0, TOKENS)
+            load_codes(wt, wq_words, g0, g1, 0, 512)
+            for g in range(g0, g1):
+                x_codes[g] = xt[:, g - g0, :]
+                w_codes[(0, g)] = wt[:, g - g0, :]
+            if s == 0:
+                load_scales(x_plane, x_scales, 0, TOKENS)
+                load_scales(planes[0], wq_scales, 0, 512)
+        for i, (words, scales, c0, c1) in enumerate(groups):
+            if i == 0:
+                continue
+            step = 4 if c1 - c0 == 512 else 2
+            for g0 in range(0, PASSES, step):
+                wt = keep.tile([P, step, 2 * (c1 - c0)], U8, name=f"w_codes{i}_{g0}", align_bytes=64)
+                load_codes(wt, words, g0, g0 + step, c0, c1)
+                for g in range(g0, g0 + step):
+                    w_codes[(i, g)] = wt[:, g - g0, :]
+                if g0 == 0:
+                    load_scales(planes[i], scales, c0, c1)
+        where = ((0, 0), (1, 0), (2, 0), (2, 512), (3, 0), (3, 512))
+
+        bias_bc = keep.tile([P, BLOCKS, NB], F32, name="bias_bc")
+        for j in range(BLOCKS):
+            bank = psum.tile([P, NB], F32, name="bank")
+            nc.tensor.matmul(
+                bank[:], lhsT=ident[:, j : j + 1].to_broadcast([P, P]), rhs=bias_rows[:], start=True, stop=True
+            )
+            nc.scalar.copy(out=bias_bc[:, j, :], in_=bank[:])
+
+        cos_rep = keep.tile([P, TILES, 2 * HEADS, HALF], F32, name="cos_rep")
+        sin_rep = keep.tile([P, TILES, HEADS, 2, HALF], F32, name="sin_rep")
+        nc.scalar.copy(out=cos_rep[:], in_=cos_sb[:].unsqueeze(2).to_broadcast([P, TILES, 2 * HEADS, HALF]))
+        sin_b = sin_sb[:].unsqueeze(2).to_broadcast([P, TILES, HEADS, HALF])
+        nc.scalar.mul(out=sin_rep[:, :, :, 0, :], in_=sin_b, mul=-1.0)
+        nc.scalar.copy(out=sin_rep[:, :, :, 1, :], in_=sin_b)
+
+        def mx_pass(bank, n, m, g):
+            grp, c0 = where[n]
+            nc.tensor.matmul_mx(
+                out=bank[:],
+                lhsT=x_codes[g][:, 2 * P * m : 2 * P * (m + 1)].bitcast(FP4X4),
+                lhsT_scale=x_plane[:, g, P * m : P * (m + 1)],
+                rhs=w_codes[(grp, g)][:, 2 * c0 : 2 * (c0 + NB)].bitcast(FP4X4),
+                rhs_scale=planes[grp][:, g, c0 : c0 + NB],
+                start=(g == 0),
+                stop=(g == PASSES - 1),
+            )
+
+        def store(dst, heads, m, src):
+            nc.sync.dma_start(
+                out=dst[0, heads : heads + HEADS, P * m : P * (m + 1), :].rearrange("h p d -> p h d"),
+                in_=src.rearrange("p (h d) -> p h d", d=HD),
+            )
+
+        def swapped_product(dst, src, m0, m1):
+            for f in range(2):
+                nc.vector.tensor_tensor(
+                    out=dst[:, m0:m1, :].rearrange("p m (h f d) -> p (m h) f d", f=2, d=HALF)[:, :, f, :],
+                    in0=src[:, m0:m1, :].rearrange("p m (h f d) -> p (m h) f d", f=2, d=HALF)[:, :, 1 - f, :],
+                    in1=sin_rep[:, m0:m1, :, :, :].rearrange("p m h f d -> p (m h) f d")[:, :, f, :],
+                    op=MULT,
+                )
+
+        cos_flat = cos_rep[:].rearrange("p m x d -> p m (x d)")
+        for n in range(BLOCKS):
+            banks = []
+            for m in range(TILES):
+                bank = psum.tile([P, NB], F32, name="bank")
+                banks.append(bank)
+            if n == 0:
+                for g in range(PASSES):
+                    for m in range(TILES):
+                        mx_pass(banks[m], n, m, g)
+            else:
+                for m in range(TILES):
+                    for g in range(PASSES):
+                        mx_pass(banks[m], n, m, g)
+
+            res = outs.tile([P, TILES, NB], F32, name="res")
+            if n == BLOCKS - 1:
+                for m in range(TILES):
+                    nc.vector.tensor_tensor(out=res[:, m, :], in0=banks[m][:], in1=bias_bc[:, n, :], op=ADD)
+                    store(out_v, 0, m, res[:, m, :])
+                continue
+
+            dst, head = (out_q, HEADS * n) if n < Q_BLOCKS else (out_k, 0)
+            biased = work.tile([P, TILES, NB], F32, name="biased")
+            prod_c = work.tile([P, TILES, NB], F32, name="prod_c")
+            prod_s = work.tile([P, TILES, NB], F32, name="prod_s")
+            for m in range(TILES):
+                nc.vector.tensor_tensor(out=biased[:, m, :], in0=banks[m][:], in1=bias_bc[:, n, :], op=ADD)
+            for m0, m1 in ((0, 2), (2, 3)):
+                nc.vector.tensor_tensor(
+                    out=prod_c[:, m0:m1, :], in0=biased[:, m0:m1, :], in1=cos_flat[:, m0:m1, :], op=MULT
+                )
+                swapped_product(prod_s, biased, m0, m1)
+            nc.vector.tensor_tensor(out=res[:, 0:2, :], in0=prod_c[:, 0:2, :], in1=prod_s[:, 0:2, :], op=ADD)
+            nc.gpsimd.tensor_tensor(out=res[:, 2, :], in0=prod_c[:, 2, :], in1=prod_s[:, 2, :], op=ADD)
+            for m in range(TILES):
+                store(dst, head, m, res[:, m, :])

@@ -22,7 +22,8 @@ HALF = 64
 Q_BLOCKS = 4
 ROPE_BLOCKS = 5
 BLOCKS = 6
-SPLITS = ((0, 1), (1, 4), (4, 8))
+SHARE = 320
+SPLITS = ((0, 2), (2, 5), (5, 8))
 
 FLOPS = 2 * TOKENS * 4096 * 3072
 
@@ -42,10 +43,10 @@ def tile_qwen2attention_pa_kernel(
             nc.sync.dma_start(out=tile[:], in_=words[g0:g1, :, 2 * c0 : 2 * c1].rearrange("g p c -> p g c"))
 
         def load_scales(plane, scales, c0, c1):
-            for quad in range(4):
+            for r in range(4):
                 nc.sync.dma_start(
-                    out=plane[32 * quad : 32 * quad + 4, :, :].bitcast(I32),
-                    in_=scales[:, 4 * quad : 4 * quad + 4, c0:c1].rearrange("g r n -> r g n").bitcast(I32),
+                    out=plane[r:P:32, :, :].bitcast(I32),
+                    in_=scales[:, r:16:4, c0:c1].rearrange("g q n -> q g n").bitcast(I32),
                 )
 
         bias_rows = keep.tile([P, NB], BF16, name="bias_rows")
@@ -67,8 +68,8 @@ def tile_qwen2attention_pa_kernel(
         for plane in planes:
             nc.vector.memset(plane[:].bitcast(I32), 0)
 
-        nc.gpsimd.dma_start(out=bias_rows[0:4, :], in_=bq.rearrange("(j n) -> j n", n=NB))
-        nc.gpsimd.dma_start(out=bias_rows[4:6, :], in_=bkv.rearrange("(j n) -> j n", n=NB))
+        nc.scalar.dma_start(out=bias_rows[0:4, :], in_=bq.rearrange("(j n) -> j n", n=NB))
+        nc.scalar.dma_start(out=bias_rows[4:6, :], in_=bkv.rearrange("(j n) -> j n", n=NB))
         make_identity(nc, ident[:])
         cos_sb = keep.tile([P, TILES, HALF], BF16, name="cos_sb")
         sin_sb = keep.tile([P, TILES, HALF], BF16, name="sin_sb")
@@ -116,35 +117,32 @@ def tile_qwen2attention_pa_kernel(
         nc.scalar.mul(out=sin_rep[:, :, :, 0, :], in_=sin_b, mul=-1.0)
         nc.scalar.copy(out=sin_rep[:, :, :, 1, :], in_=sin_b)
 
-        def mx_pass(bank, n, m, g):
+        def mx_pass(bank, n, m, g, cut, width):
             grp, c0 = where[n]
+            c0 += cut
             nc.tensor.matmul_mx(
-                out=bank[:],
+                out=bank[:, 0:width],
                 lhsT=x_codes[g][:, 2 * P * m : 2 * P * (m + 1)].bitcast(FP4X4),
                 lhsT_scale=x_plane[:, g, P * m : P * (m + 1)],
-                rhs=w_codes[(grp, g)][:, 2 * c0 : 2 * (c0 + NB)].bitcast(FP4X4),
-                rhs_scale=planes[grp][:, g, c0 : c0 + NB],
+                rhs=w_codes[(grp, g)][:, 2 * c0 : 2 * (c0 + width)].bitcast(FP4X4),
+                rhs_scale=planes[grp][:, g, c0 : c0 + width],
                 start=(g == 0),
                 stop=(g == PASSES - 1),
             )
 
-        def store(dst, heads, m, src):
+        def store(dst, heads, m, src, count=HEADS):
             nc.sync.dma_start(
-                out=dst[0, heads : heads + HEADS, P * m : P * (m + 1), :].rearrange("h p d -> p h d"),
+                out=dst[0, heads : heads + count, P * m : P * (m + 1), :].rearrange("h p d -> p h d"),
                 in_=src.rearrange("p (h d) -> p h d", d=HD),
             )
 
-        def swapped_product(dst, src, m0, m1):
-            for f in range(2):
-                nc.vector.tensor_tensor(
-                    out=dst[:, m0:m1, :].rearrange("p m (h f d) -> p (m h) f d", f=2, d=HALF)[:, :, f, :],
-                    in0=src[:, m0:m1, :].rearrange("p m (h f d) -> p (m h) f d", f=2, d=HALF)[:, :, 1 - f, :],
-                    in1=sin_rep[:, m0:m1, :, :, :].rearrange("p m h f d -> p (m h) f d")[:, :, f, :],
-                    op=MULT,
-                )
-
         cos_flat = cos_rep[:].rearrange("p m x d -> p m (x d)")
-        for n in range(BLOCKS):
+        sin_flat = sin_rep[:].rearrange("p m h f d -> p m (h f d)")
+
+        def halves(ap):
+            return ap.rearrange("p m (h f d) -> p (m h) f d", f=2, d=HALF)
+
+        for n in range(ROPE_BLOCKS):
             banks = []
             for m in range(TILES):
                 bank = psum.tile([P, NB], F32, name="bank")
@@ -152,20 +150,14 @@ def tile_qwen2attention_pa_kernel(
             if n == 0:
                 for g in range(PASSES):
                     for m in range(TILES):
-                        mx_pass(banks[m], n, m, g)
+                        mx_pass(banks[m], n, m, g, 0, NB)
             else:
                 for m in range(TILES):
                     for g in range(PASSES):
-                        mx_pass(banks[m], n, m, g)
-
-            res = outs.tile([P, TILES, NB], F32, name="res")
-            if n == BLOCKS - 1:
-                for m in range(TILES):
-                    nc.vector.tensor_tensor(out=res[:, m, :], in0=banks[m][:], in1=bias_bc[:, n, :], op=ADD)
-                    store(out_v, 0, m, res[:, m, :])
-                continue
+                        mx_pass(banks[m], n, m, g, 0, NB)
 
             dst, head = (out_q, HEADS * n) if n < Q_BLOCKS else (out_k, 0)
+            res = outs.tile([P, TILES, NB], F32, name="res")
             biased = work.tile([P, TILES, NB], F32, name="biased")
             prod_c = work.tile([P, TILES, NB], F32, name="prod_c")
             prod_s = work.tile([P, TILES, NB], F32, name="prod_s")
@@ -175,8 +167,29 @@ def tile_qwen2attention_pa_kernel(
                 nc.vector.tensor_tensor(
                     out=prod_c[:, m0:m1, :], in0=biased[:, m0:m1, :], in1=cos_flat[:, m0:m1, :], op=MULT
                 )
-                swapped_product(prod_s, biased, m0, m1)
-            nc.vector.tensor_tensor(out=res[:, 0:2, :], in0=prod_c[:, 0:2, :], in1=prod_s[:, 0:2, :], op=ADD)
-            nc.gpsimd.tensor_tensor(out=res[:, 2, :], in0=prod_c[:, 2, :], in1=prod_s[:, 2, :], op=ADD)
+                nc.vector.tensor_tensor(
+                    out=halves(prod_s[:, m0:m1, :]),
+                    in0=halves(biased[:, m0:m1, :])[:, :, ::-1, :],
+                    in1=halves(sin_flat[:, m0:m1, :]),
+                    op=MULT,
+                )
+            for m0, m1 in ((0, 2), (2, 3)):
+                nc.vector.tensor_tensor(
+                    out=res[:, m0:m1, 0:SHARE], in0=prod_c[:, m0:m1, 0:SHARE], in1=prod_s[:, m0:m1, 0:SHARE], op=ADD
+                )
+            nc.gpsimd.tensor_tensor(
+                out=res[:, :, SHARE:NB], in0=prod_c[:, :, SHARE:NB], in1=prod_s[:, :, SHARE:NB], op=ADD
+            )
             for m in range(TILES):
                 store(dst, head, m, res[:, m, :])
+
+        n = BLOCKS - 1
+        for m, cut, width in ((0, 0, NB), (1, 0, NB), (2, 0, NB // 2), (2, NB // 2, NB // 2)):
+            bank = psum.tile([P, NB], F32, name="bank")
+            for g in range(PASSES):
+                mx_pass(bank, n, m, g, cut, width)
+            value = outs.tile([P, NB], F32, name="value")
+            nc.vector.tensor_tensor(
+                out=value[:, 0:width], in0=bank[:, 0:width], in1=bias_bc[:, n, cut : cut + width], op=ADD
+            )
+            store(out_v, cut // HD, m, value[:, 0:width], width // HD)

@@ -51,7 +51,7 @@ def tile_qwen2attention_pa_kernel(
 
         bias_rows = keep.tile([P, NB], BF16, name="bias_rows")
         ident = keep.tile([P, P], BF16, name="ident")
-        x_plane = keep.tile([P, PASSES, TOKENS], U8, name="x_plane", align_bytes=64)
+        x_plane = keep.tile([P, PASSES, TOKENS], U8, name="x_plane", align_bytes=256)
         groups = (
             (wq_words, wq_scales, 0, 512),
             (wq_words, wq_scales, 512, 1024),
@@ -60,7 +60,7 @@ def tile_qwen2attention_pa_kernel(
         )
         planes = []
         for i, (words, scales, c0, c1) in enumerate(groups):
-            plane = keep.tile([P, PASSES, c1 - c0], U8, name=f"plane{i}", align_bytes=64)
+            plane = keep.tile([P, PASSES, c1 - c0], U8, name=f"plane{i}", align_bytes=256)
             planes.append(plane)
 
         nc.vector.memset(bias_rows[:], 0.0)
@@ -79,12 +79,16 @@ def tile_qwen2attention_pa_kernel(
         x_codes = {}
         w_codes = {}
         for s, (g0, g1) in enumerate(SPLITS):
-            xt = keep.tile([P, g1 - g0, 2 * TOKENS], U8, name=f"x_codes{s}", align_bytes=64)
-            wt = keep.tile([P, g1 - g0, 2 * 512], U8, name=f"w_codes0_{s}", align_bytes=64)
-            load_codes(xt, x_words, g0, g1, 0, TOKENS)
+            xa = keep.tile([P, g1 - g0, 2 * 256], U8, name=f"x_codes_a{s}", align_bytes=256)
+            xb = keep.tile([P, g1 - g0, 2 * 128], U8, name=f"x_codes_b{s}", align_bytes=256)
+            wt = keep.tile([P, g1 - g0, 2 * 512], U8, name=f"w_codes0_{s}", align_bytes=256)
+            load_codes(xa, x_words, g0, g1, 0, 256)
             load_codes(wt, wq_words, g0, g1, 0, 512)
+            load_codes(xb, x_words, g0, g1, 256, 384)
             for g in range(g0, g1):
-                x_codes[g] = xt[:, g - g0, :]
+                x_codes[(0, g)] = xa[:, g - g0, 0:256]
+                x_codes[(1, g)] = xa[:, g - g0, 256:512]
+                x_codes[(2, g)] = xb[:, g - g0, :]
                 w_codes[(0, g)] = wt[:, g - g0, :]
             if s == 0:
                 load_scales(x_plane, x_scales, 0, TOKENS)
@@ -94,7 +98,7 @@ def tile_qwen2attention_pa_kernel(
                 continue
             step = 4 if c1 - c0 == 512 else 2
             for g0 in range(0, PASSES, step):
-                wt = keep.tile([P, step, 2 * (c1 - c0)], U8, name=f"w_codes{i}_{g0}", align_bytes=64)
+                wt = keep.tile([P, step, 2 * (c1 - c0)], U8, name=f"w_codes{i}_{g0}", align_bytes=256)
                 load_codes(wt, words, g0, g0 + step, c0, c1)
                 for g in range(g0, g0 + step):
                     w_codes[(i, g)] = wt[:, g - g0, :]
@@ -122,7 +126,7 @@ def tile_qwen2attention_pa_kernel(
             c0 += cut
             nc.tensor.matmul_mx(
                 out=bank[:, 0:width],
-                lhsT=x_codes[g][:, 2 * P * m : 2 * P * (m + 1)].bitcast(FP4X4),
+                lhsT=x_codes[(m, g)].bitcast(FP4X4),
                 lhsT_scale=x_plane[:, g, P * m : P * (m + 1)],
                 rhs=w_codes[(grp, g)][:, 2 * c0 : 2 * (c0 + width)].bitcast(FP4X4),
                 rhs_scale=planes[grp][:, g, c0 : c0 + width],
@@ -147,14 +151,13 @@ def tile_qwen2attention_pa_kernel(
             for m in range(TILES):
                 bank = psum.tile([P, NB], F32, name="bank")
                 banks.append(bank)
-            if n == 0:
-                for g in range(PASSES):
-                    for m in range(TILES):
-                        mx_pass(banks[m], n, m, g, 0, NB)
-            else:
+            outer = (6, 4, 4, 0, 0)[n]
+            for g in range(outer):
                 for m in range(TILES):
-                    for g in range(PASSES):
-                        mx_pass(banks[m], n, m, g, 0, NB)
+                    mx_pass(banks[m], n, m, g, 0, NB)
+            for m in range(TILES):
+                for g in range(outer, PASSES):
+                    mx_pass(banks[m], n, m, g, 0, NB)
 
             dst, head = (out_q, HEADS * n) if n < Q_BLOCKS else (out_k, 0)
             res = outs.tile([P, TILES, NB], F32, name="res")

@@ -22,7 +22,7 @@ HALF = 64
 Q_BLOCKS = 4
 ROPE_BLOCKS = 5
 BLOCKS = 6
-SHARE = 320
+SHARES = (256, 256, 256, 384)
 SPLITS = ((0, 2), (2, 5), (5, 8))
 
 FLOPS = 2 * TOKENS * 4096 * 3072
@@ -146,48 +146,46 @@ def tile_qwen2attention_pa_kernel(
         def halves(ap):
             return ap.rearrange("p m (h f d) -> p (m h) f d", f=2, d=HALF)
 
-        for n in range(ROPE_BLOCKS):
+        def bank_passes(n, outer):
             banks = []
             for m in range(TILES):
                 bank = psum.tile([P, NB], F32, name="bank")
                 banks.append(bank)
-            outer = (6, 4, 4, 0, 0)[n]
             for g in range(outer):
                 for m in range(TILES):
                     mx_pass(banks[m], n, m, g, 0, NB)
             for m in range(TILES):
                 for g in range(outer, PASSES):
                     mx_pass(banks[m], n, m, g, 0, NB)
+            return banks
 
-            dst, head = (out_q, HEADS * n) if n < Q_BLOCKS else (out_k, 0)
-            res = outs.tile([P, TILES, NB], F32, name="res")
-            biased = work.tile([P, TILES, NB], F32, name="biased")
-            prod_c = work.tile([P, TILES, NB], F32, name="prod_c")
-            prod_s = work.tile([P, TILES, NB], F32, name="prod_s")
-            for m in range(TILES):
-                nc.vector.tensor_tensor(out=biased[:, m, :], in0=banks[m][:], in1=bias_bc[:, n, :], op=ADD)
-            for m0, m1 in ((0, 2), (2, 3)):
-                nc.vector.tensor_tensor(
-                    out=prod_c[:, m0:m1, :], in0=biased[:, m0:m1, :], in1=cos_flat[:, m0:m1, :], op=MULT
-                )
-                nc.vector.tensor_tensor(
-                    out=halves(prod_s[:, m0:m1, :]),
-                    in0=halves(biased[:, m0:m1, :])[:, :, ::-1, :],
-                    in1=halves(sin_flat[:, m0:m1, :]),
-                    op=MULT,
-                )
-            for m0, m1 in ((0, 2), (2, 3)):
-                nc.vector.tensor_tensor(
-                    out=res[:, m0:m1, 0:SHARE], in0=prod_c[:, m0:m1, 0:SHARE], in1=prod_s[:, m0:m1, 0:SHARE], op=ADD
-                )
-            nc.gpsimd.tensor_tensor(
-                out=res[:, :, SHARE:NB], in0=prod_c[:, :, SHARE:NB], in1=prod_s[:, :, SHARE:NB], op=ADD
+        def add_bias(n, m):
+            nc.vector.tensor_tensor(out=biased[n][:, m, :], in0=banks[n][m][:], in1=bias_bc[:, n, :], op=ADD)
+
+        def times_cos(n, m0, m1):
+            nc.vector.tensor_tensor(
+                out=prod_c[n][:, m0:m1, :], in0=biased[n][:, m0:m1, :], in1=cos_flat[:, m0:m1, :], op=MULT
             )
-            for m in range(TILES):
-                store(dst, head, m, res[:, m, :])
 
-        n = BLOCKS - 1
-        for m, cut, width in ((0, 0, NB), (1, 0, NB), (2, 0, NB // 2), (2, NB // 2, NB // 2)):
+        def times_sin(n, m0, m1):
+            nc.vector.tensor_tensor(
+                out=halves(prod_s[n][:, m0:m1, :]),
+                in0=halves(biased[n][:, m0:m1, :])[:, :, ::-1, :],
+                in1=halves(sin_flat[:, m0:m1, :]),
+                op=MULT,
+            )
+
+        def add_products(engine, n, m0, m1, c0, c1):
+            engine.tensor_tensor(
+                out=res[n][:, m0:m1, c0:c1], in0=prod_c[n][:, m0:m1, c0:c1], in1=prod_s[n][:, m0:m1, c0:c1], op=ADD
+            )
+
+        def store_rope(n, m):
+            dst, head = (out_q, HEADS * n) if n < Q_BLOCKS else (out_k, 0)
+            store(dst, head, m, res[n][:, m, :])
+
+        def value_part(m, cut, width):
+            n = BLOCKS - 1
             bank = psum.tile([P, NB], F32, name="bank")
             for g in range(PASSES):
                 mx_pass(bank, n, m, g, cut, width)
@@ -196,3 +194,50 @@ def tile_qwen2attention_pa_kernel(
                 out=value[:, 0:width], in0=bank[:, 0:width], in1=bias_bc[:, n, cut : cut + width], op=ADD
             )
             store(out_v, cut // HD, m, value[:, 0:width], width // HD)
+
+        banks, biased, prod_c, prod_s, res = {}, {}, {}, {}, {}
+        for n in range(ROPE_BLOCKS):
+            banks[n] = bank_passes(n, (6, 4, 4, 0, 0)[n])
+            b_tile = work.tile([P, TILES, NB], F32, name="b_tile")
+            c_tile = work.tile([P, TILES, NB], F32, name="c_tile")
+            s_tile = work.tile([P, TILES, NB], F32, name="s_tile")
+            r_tile = outs.tile([P, TILES, NB], F32, name="r_tile")
+            biased[n], prod_c[n], prod_s[n], res[n] = b_tile, c_tile, s_tile, r_tile
+
+            def finish(k):
+                share = SHARES[k]
+                add_products(nc.gpsimd, k, 0, TILES, share, NB)
+                add_products(nc.vector, k, 0, TILES, 0, share)
+                for m in range(TILES):
+                    store_rope(k, m)
+
+            if n < ROPE_BLOCKS - 1:
+                for m in range(TILES):
+                    add_bias(n, m)
+                if n > 0:
+                    finish(n - 1)
+                    times_cos(n, 0, TILES)
+                else:
+                    times_cos(n, 0, 2)
+                    times_cos(n, 2, TILES)
+                times_sin(n, 0, TILES)
+            else:
+                add_bias(n, 0)
+                add_bias(n, 1)
+                finish(n - 1)
+                times_cos(n, 0, 2)
+                add_bias(n, 2)
+                times_sin(n, 0, 2)
+                add_products(nc.gpsimd, n, 0, 2, 384, NB)
+                value_part(0, 0, NB)
+                add_products(nc.vector, n, 0, 2, 0, 384)
+                store_rope(n, 0)
+                store_rope(n, 1)
+                times_cos(n, 2, TILES)
+                times_sin(n, 2, TILES)
+                add_products(nc.gpsimd, n, 2, TILES, 256, NB)
+                value_part(1, 0, NB)
+                add_products(nc.vector, n, 2, TILES, 0, 256)
+                store_rope(n, 2)
+                value_part(2, 0, NB // 2)
+                value_part(2, NB // 2, NB // 2)

from contextlib import ExitStack

import concourse.mybir as mybir
from concourse.masks import make_identity

F32 = mybir.dt.float32
BF16 = mybir.dt.bfloat16
I32 = mybir.dt.int32
U8 = mybir.dt.uint8
FP4X4 = mybir.dt.float4_e2m1fn_x4
ADD = mybir.AluOpType.add
MULT = mybir.AluOpType.mult

P = 128
PASSES = 8
TOKENS = 384
TILES = 3
NB = 512
HEADS = 4
HD = 128
HALF = 64
Q_BLOCKS = 4
ROPE_BLOCKS = 5
BLOCKS = 6
SHARES = (256, 256, 256, 384)
SPLITS = ((0, 2), (2, 5), (5, 8))

FLOPS = 2 * TOKENS * 4096 * 3072


def tile_qwen2attention_pa_kernel(
    tc, x_words, x_scales, wq_words, wq_scales, bq, wkv_words, wkv_scales, bkv, cos, sin, out_q, out_k, out_v
):
    nc = tc.nc
    with ExitStack() as ctx:
        keep = ctx.enter_context(tc.tile_pool(name="keep", bufs=1))
        work = ctx.enter_context(tc.tile_pool(name="work", bufs=2))
        outs = ctx.enter_context(tc.tile_pool(name="outs", bufs=6))
        psum = ctx.enter_context(tc.psum_pool(name="psum", bufs=8))
        ctx.enter_context(tc.manual_schedule())

        def load_codes(tile, words, g0, g1, c0, c1):
            nc.sync.dma_start(out=tile[:], in_=words[g0:g1, :, 2 * c0 : 2 * c1].rearrange("g p c -> p g c"))

        def load_scales(plane, scales, c0, c1):
            for r in range(4):
                nc.sync.dma_start(
                    out=plane[r:P:32, :, :].bitcast(I32),
                    in_=scales[:, r:16:4, c0:c1].rearrange("g q n -> q g n").bitcast(I32),
                )

        bias_rows = keep.tile([P, NB], BF16, name="bias_rows")
        ident = keep.tile([P, P], BF16, name="ident")
        x_plane = keep.tile([P, PASSES, TOKENS], U8, name="x_plane", align_bytes=256)
        groups = (
            (wq_words, wq_scales, 0, 512),
            (wq_words, wq_scales, 512, 1024),
            (wq_words, wq_scales, 1024, 2048),
            (wkv_words, wkv_scales, 0, 1024),
        )
        planes = []
        for i, (words, scales, c0, c1) in enumerate(groups):
            plane = keep.tile([P, PASSES, c1 - c0], U8, name=f"plane{i}", align_bytes=256)
            planes.append(plane)

        nc.vector.memset(bias_rows[:], 0.0)
        nc.vector.memset(x_plane[:].bitcast(I32), 0)
        for plane in planes:
            nc.vector.memset(plane[:].bitcast(I32), 0)

        nc.scalar.dma_start(out=bias_rows[0:4, :], in_=bq.rearrange("(j n) -> j n", n=NB))
        nc.scalar.dma_start(out=bias_rows[4:6, :], in_=bkv.rearrange("(j n) -> j n", n=NB))
        make_identity(nc, ident[:])
        cos_sb = keep.tile([P, TILES, HALF], BF16, name="cos_sb")
        sin_sb = keep.tile([P, TILES, HALF], BF16, name="sin_sb")
        nc.gpsimd.dma_start(out=cos_sb[:], in_=cos.rearrange("(m p) d -> p m d", p=P))
        nc.gpsimd.dma_start(out=sin_sb[:], in_=sin.rearrange("(m p) d -> p m d", p=P))

        x_codes = {}
        w_codes = {}
        for s, (g0, g1) in enumerate(SPLITS):
            xa = keep.tile([P, g1 - g0, 2 * 256], U8, name=f"x_codes_a{s}", align_bytes=256)
            xb = keep.tile([P, g1 - g0, 2 * 128], U8, name=f"x_codes_b{s}", align_bytes=256)
            wt = keep.tile([P, g1 - g0, 2 * 512], U8, name=f"w_codes0_{s}", align_bytes=256)
            load_codes(xa, x_words, g0, g1, 0, 256)
            load_codes(wt, wq_words, g0, g1, 0, 512)
            load_codes(xb, x_words, g0, g1, 256, 384)
            for g in range(g0, g1):
                x_codes[(0, g)] = xa[:, g - g0, 0:256]
                x_codes[(1, g)] = xa[:, g - g0, 256:512]
                x_codes[(2, g)] = xb[:, g - g0, :]
                w_codes[(0, g)] = wt[:, g - g0, :]
            if s == 0:
                load_scales(x_plane, x_scales, 0, TOKENS)
                load_scales(planes[0], wq_scales, 0, 512)
        for i, (words, scales, c0, c1) in enumerate(groups):
            if i == 0:
                continue
            step = 4 if c1 - c0 == 512 else 2
            for g0 in range(0, PASSES, step):
                wt = keep.tile([P, step, 2 * (c1 - c0)], U8, name=f"w_codes{i}_{g0}", align_bytes=256)
                load_codes(wt, words, g0, g0 + step, c0, c1)
                for g in range(g0, g0 + step):
                    w_codes[(i, g)] = wt[:, g - g0, :]
                if g0 == 0:
                    load_scales(planes[i], scales, c0, c1)
        where = ((0, 0), (1, 0), (2, 0), (2, 512), (3, 0), (3, 512))

        bias_bc = keep.tile([P, BLOCKS, NB], F32, name="bias_bc")
        for j in range(BLOCKS):
            bank = psum.tile([P, NB], F32, name="bank")
            nc.tensor.matmul(
                bank[:], lhsT=ident[:, j : j + 1].to_broadcast([P, P]), rhs=bias_rows[:], start=True, stop=True
            )
            nc.scalar.copy(out=bias_bc[:, j, :], in_=bank[:])

        cos_rep = keep.tile([P, TILES, 2 * HEADS, HALF], F32, name="cos_rep")
        sin_rep = keep.tile([P, TILES, HEADS, 2, HALF], F32, name="sin_rep")
        nc.scalar.copy(out=cos_rep[:], in_=cos_sb[:].unsqueeze(2).to_broadcast([P, TILES, 2 * HEADS, HALF]))
        sin_b = sin_sb[:].unsqueeze(2).to_broadcast([P, TILES, HEADS, HALF])
        nc.scalar.mul(out=sin_rep[:, :, :, 0, :], in_=sin_b, mul=-1.0)
        nc.scalar.copy(out=sin_rep[:, :, :, 1, :], in_=sin_b)

        def mx_pass(bank, n, m, g, cut, width):
            grp, c0 = where[n]
            c0 += cut
            nc.tensor.matmul_mx(
                out=bank[:, 0:width],
                lhsT=x_codes[(m, g)].bitcast(FP4X4),
                lhsT_scale=x_plane[:, g, P * m : P * (m + 1)],
                rhs=w_codes[(grp, g)][:, 2 * c0 : 2 * (c0 + width)].bitcast(FP4X4),
                rhs_scale=planes[grp][:, g, c0 : c0 + width],
                start=(g == 0),
                stop=(g == PASSES - 1),
            )

        def store(dst, heads, m, src, count=HEADS):
            nc.sync.dma_start(
                out=dst[0, heads : heads + count, P * m : P * (m + 1), :].rearrange("h p d -> p h d"),
                in_=src.rearrange("p (h d) -> p h d", d=HD),
            )

        cos_flat = cos_rep[:].rearrange("p m x d -> p m (x d)")
        sin_flat = sin_rep[:].rearrange("p m h f d -> p m (h f d)")

        def halves(ap):
            return ap.rearrange("p m (h f d) -> p (m h) f d", f=2, d=HALF)

        def bank_passes(n, outer):
            banks = []
            for m in range(TILES):
                bank = psum.tile([P, NB], F32, name="bank")
                banks.append(bank)
            for g in range(outer):
                for m in range(TILES):
                    mx_pass(banks[m], n, m, g, 0, NB)
            for m in range(TILES):
                for g in range(outer, PASSES):
                    mx_pass(banks[m], n, m, g, 0, NB)
            return banks

        def add_bias(n, m):
            nc.vector.tensor_tensor(out=biased[n][:, m, :], in0=banks[n][m][:], in1=bias_bc[:, n, :], op=ADD)

        def times_cos(n, m0, m1):
            nc.vector.tensor_tensor(
                out=prod_c[n][:, m0:m1, :], in0=biased[n][:, m0:m1, :], in1=cos_flat[:, m0:m1, :], op=MULT
            )

        def times_sin(n, m0, m1):
            nc.vector.tensor_tensor(
                out=halves(prod_s[n][:, m0:m1, :]),
                in0=halves(biased[n][:, m0:m1, :])[:, :, ::-1, :],
                in1=halves(sin_flat[:, m0:m1, :]),
                op=MULT,
            )

        def add_products(engine, n, m0, m1, c0, c1):
            engine.tensor_tensor(
                out=res[n][:, m0:m1, c0:c1], in0=prod_c[n][:, m0:m1, c0:c1], in1=prod_s[n][:, m0:m1, c0:c1], op=ADD
            )

        def store_rope(n, m):
            dst, head = (out_q, HEADS * n) if n < Q_BLOCKS else (out_k, 0)
            store(dst, head, m, res[n][:, m, :])

        def value_part(m, cut, width):
            n = BLOCKS - 1
            bank = psum.tile([P, NB], F32, name="bank")
            for g in range(PASSES):
                mx_pass(bank, n, m, g, cut, width)
            value = outs.tile([P, NB], F32, name="value")
            nc.vector.tensor_tensor(
                out=value[:, 0:width], in0=bank[:, 0:width], in1=bias_bc[:, n, cut : cut + width], op=ADD
            )
            store(out_v, cut // HD, m, value[:, 0:width], width // HD)

        banks, biased, prod_c, prod_s, res = {}, {}, {}, {}, {}
        for n in range(ROPE_BLOCKS):
            banks[n] = bank_passes(n, (6, 4, 4, 0, 0)[n])
            b_tile = work.tile([P, TILES, NB], F32, name="b_tile")
            c_tile = work.tile([P, TILES, NB], F32, name="c_tile")
            s_tile = work.tile([P, TILES, NB], F32, name="s_tile")
            r_tile = outs.tile([P, TILES, NB], F32, name="r_tile")
            biased[n], prod_c[n], prod_s[n], res[n] = b_tile, c_tile, s_tile, r_tile

            def finish(k):
                share = SHARES[k]
                add_products(nc.gpsimd, k, 0, TILES, share, NB)
                add_products(nc.vector, k, 0, TILES, 0, share)
                for m in range(TILES):
                    store_rope(k, m)

            if n < ROPE_BLOCKS - 1:
                for m in range(TILES):
                    add_bias(n, m)
                if n > 0:
                    finish(n - 1)
                    times_cos(n, 0, TILES)
                else:
                    times_cos(n, 0, 2)
                    times_cos(n, 2, TILES)
                times_sin(n, 0, TILES)
            else:
                add_bias(n, 0)
                add_bias(n, 1)
                finish(n - 1)
                times_cos(n, 0, 2)
                add_bias(n, 2)
                times_sin(n, 0, 2)
                add_products(nc.gpsimd, n, 0, 2, 384, NB)
                value_part(0, 0, NB)
                add_products(nc.vector, n, 0, 2, 0, 384)
                store_rope(n, 0)
                store_rope(n, 1)
                times_cos(n, 2, TILES)
                times_sin(n, 2, TILES)
                add_products(nc.gpsimd, n, 2, TILES, 256, NB)
                value_part(1, 0, NB)
                add_products(nc.vector, n, 2, TILES, 0, 256)
                store_rope(n, 2)
                value_part(2, 0, NB // 2)
                value_part(2, NB // 2, NB // 2)
